import numpy as np
import ml_dtypes


def mxq(x, axis, fmt="e4m3"):
    dtype, down = {"e4m3": (ml_dtypes.float8_e4m3fn, 7), "e5m2": (ml_dtypes.float8_e5m2, 14)}[fmt]
    v = np.moveaxis(np.asarray(x, np.float32).astype(ml_dtypes.bfloat16).astype(np.float64), axis, -1)
    blocks = v.reshape(v.shape[:-1] + (-1, 32))
    amax = np.abs(blocks).max(-1, keepdims=True)
    byte = np.maximum(np.where(amax > 0, np.frexp(amax)[1] - 1 + 127, 0) - down, 1)
    scale = np.exp2(byte - 127.0)
    codes = (blocks / scale).astype(np.float32).astype(dtype).astype(np.float64)
    return np.moveaxis((codes * scale).reshape(v.shape), -1, axis)


WIDE = False


def mx_kscale(k):
    if not WIDE:
        return np.ones(k)
    levels = np.array([10, -10, 5, -5, 0])
    a = np.random.permutation(np.resize(levels, k // 512 * 4)).reshape(k // 512, 4)
    idx = np.arange(k)
    return np.exp2(a[idx // 512, idx % 128 // 32])


BF16 = ml_dtypes.bfloat16


def bf(x):
    return np.asarray(x, np.float32).astype(BF16)


def f64(x):
    return np.asarray(x).astype(np.float64)


B, I, H = 128, 512, 512
EPS = 1e-12
FORGET_BIAS = 1.0


def layer_norm(x, g, b):
    mean = np.mean(x, axis=-1, keepdims=True)
    var = np.mean((x - mean) ** 2, axis=-1, keepdims=True)
    var_filter = 0.01 * (var < EPS).astype(np.float64)
    normalized = (x - mean) / np.sqrt(var + EPS + var_filter)
    return g * normalized + b


def sigmoid(v):
    return 1.0 / (1.0 + np.exp(-v))


def setup_inputs():
    s, t = mx_kscale(I), mx_kscale(H)
    return {"x": bf(np.random.standard_normal((B, I)) * s),
            "hx": bf(np.random.standard_normal((B, H)) * t),
            "cx": bf(np.random.standard_normal((B, H))),
            "weight_ih": bf(np.random.standard_normal((4 * H, I)) / np.sqrt(I) / s[None, :]),
            "weight_hh": bf(np.random.standard_normal((4 * H, H)) / np.sqrt(H) / t[None, :]),
            "gamma": bf(1.0 + 0.1 * np.random.standard_normal((5, H))),
            "beta": bf(0.1 * np.random.standard_normal((5, H)))}


def reference(x, hx, cx, weight_ih, weight_hh, gamma, beta):
    cx, gamma, beta = f64(cx), f64(gamma), f64(beta)
    gates = (mxq(f64(x), 1, "e4m3") @ mxq(f64(weight_ih), 1, "e4m3").T) + (mxq(f64(hx), 1, "e4m3") @ mxq(f64(weight_hh), 1, "e4m3").T)
    ingate, forgetgate, cellgate, outgate = np.split(gates, 4, axis=1)
    ingate = layer_norm(ingate, gamma[0], beta[0])
    forgetgate = layer_norm(forgetgate, gamma[1], beta[1])
    cellgate = layer_norm(cellgate, gamma[2], beta[2])
    outgate = layer_norm(outgate, gamma[3], beta[3])
    ingate = sigmoid(ingate)
    forgetgate = sigmoid(forgetgate + FORGET_BIAS)
    cellgate = np.tanh(cellgate)
    outgate = sigmoid(outgate)
    cy = forgetgate * cx + ingate * cellgate
    cy = layer_norm(cy, gamma[4], beta[4])
    hy = outgate * np.tanh(cy)
    hy_dropped = hy
    return (hy_dropped, hy, cy)

@@ -1,0 +1,203 @@
+from contextlib import ExitStack
+
+import concourse.mybir as mybir
+from concourse.masks import make_identity
+
+F32 = mybir.dt.float32
+BF16 = mybir.dt.bfloat16
+U32 = mybir.dt.uint32
+U8 = mybir.dt.uint8
+FP8X4 = mybir.dt.float8_e4m3fn_x4
+ALU = mybir.AluOpType
+ACT = mybir.ActivationFunctionType
+
+P = 128
+K = 512
+H = 512
+WORDS = K // 2
+ROW_BLOCKS = H // P
+NORMS = 5
+EPS = 1e-12
+VAR_FLOOR = 0.01
+FORGET_BIAS = 1.0
+
+FLOPS = 2 * P * (4 * H) * (2 * K)
+
+
+def tile_layernormdropoutlstmcell_s_kernel(
+    tc, x, hx, cx, weight_ih, weight_hh, gamma, beta, out_0, out_1, out_2
+):
+    nc = tc.nc
+    with ExitStack() as ctx:
+        consts = ctx.enter_context(tc.tile_pool(name="consts", bufs=1))
+        inputs = ctx.enter_context(tc.tile_pool(name="inputs", bufs=1))
+        staging = ctx.enter_context(tc.tile_pool(name="staging", bufs=3))
+        operands = ctx.enter_context(tc.tile_pool(name="operands", bufs=1))
+        kept = ctx.enter_context(tc.tile_pool(name="kept", bufs=1))
+        work = ctx.enter_context(tc.tile_pool(name="work", bufs=2))
+        banks = ctx.enter_context(tc.psum_pool(name="banks", bufs=4))
+        sums = ctx.enter_context(tc.psum_pool(name="sums", bufs=4))
+
+        affine_rows = consts.tile([P, H], BF16)
+        nc.vector.memset(affine_rows[:], 0.0)
+        minus_half = consts.tile([P, 1], F32)
+        nc.vector.memset(minus_half[:], -0.5)
+        forget_bias = consts.tile([P, 1], F32)
+        nc.vector.memset(forget_bias[:], FORGET_BIAS)
+        ident = consts.tile([P, P], F32)
+        make_identity(nc, ident[:])
+
+        nc.scalar.dma_start(out=affine_rows[0:NORMS, :], in_=gamma[:, :])
+        nc.scalar.dma_start(out=affine_rows[NORMS : 2 * NORMS, :], in_=beta[:, :])
+        cx_rows = inputs.tile([P, H], BF16)
+        nc.scalar.dma_start(out=cx_rows[:], in_=cx[:, :])
+        x_rows = inputs.tile([P, K], BF16)
+        nc.sync.dma_start(out=x_rows[:], in_=x[:, :])
+        hx_rows = inputs.tile([P, K], BF16)
+        nc.sync.dma_start(out=hx_rows[:], in_=hx[:, :])
+        w_rows = {}
+        for g in range(4):
+            for m, weight in enumerate((weight_ih, weight_hh)):
+                rows = inputs.tile([P, ROW_BLOCKS * K], BF16, name="w_rows_%d_%d" % (g, m))
+                nc.sync.dma_start(
+                    out=rows[:].rearrange("p (b k) -> p b k", b=ROW_BLOCKS),
+                    in_=weight[g * H : (g + 1) * H, :].rearrange("(b p) k -> p b k", p=P),
+                )
+                w_rows[(g, m)] = rows
+
+        table_warm = consts.tile([P, 1], F32)
+        nc.scalar.activation(out=table_warm[:], in_=forget_bias[:], func=ACT.Sigmoid)
+
+        def transpose_words(bank_planes, column, rows_words):
+            for u in range(2):
+                nc.tensor.transpose(
+                    bank_planes[:, u, column : column + P],
+                    rows_words[:, u * P : (u + 1) * P],
+                    ident[:],
+                )
+
+        def regroup(grouped_words, bank_planes):
+            nc.scalar.copy(
+                out=grouped_words.rearrange("p (c u) -> p c u", u=2),
+                in_=bank_planes.rearrange("p u c -> p c u"),
+            )
+
+        bank = banks.tile([P, 512], F32, name="bank")
+        transpose_words(bank[:].rearrange("p (u c) -> p u c", u=2), 0, affine_rows[:].bitcast(F32))
+        affine_cols = consts.tile([P, 2, 2 * NORMS], F32)
+        nc.vector.tensor_copy(
+            out=affine_cols[:],
+            in_=bank[:].rearrange("p (u c) -> p u c", u=2)[:, :, 0 : 2 * NORMS],
+        )
+        affine = []
+        for n in range(NORMS):
+            bank = banks.tile([P, 512], F32, name="bank")
+            for s in range(2):
+                for u in range(2):
+                    column = (2 * s + u) * P
+                    row = s * NORMS + n
+                    nc.tensor.transpose(
+                        bank[:, column : column + P],
+                        affine_cols[:, u, row : row + 1].to_broadcast([P, P]),
+                        ident[:],
+                    )
+            spread = consts.tile([P, 2 * H], BF16, name="affine_%d" % n)
+            nc.scalar.copy(out=spread[:].bitcast(F32), in_=bank[:])
+            affine.append(spread)
+
+        bank = banks.tile([P, 512], F32, name="bank")
+        planes = bank[:].rearrange("p (u c) -> p u c", u=2)
+        transpose_words(planes, 0, x_rows[:].bitcast(F32))
+        transpose_words(planes, P, hx_rows[:].bitcast(F32))
+        act_grouped = staging.tile([P, 4 * 2 * P], BF16, align_bytes=64)
+        regroup(act_grouped[:].bitcast(F32), planes)
+        act_codes = operands.tile([P, 2 * P], U32, align_bytes=64)
+        act_scales = operands.tile([P, 2 * P], U8, align_bytes=64)
+        nc.vector.quantize_mx(
+            out=act_codes[:].bitcast(FP8X4), scales=act_scales[:], in_=act_grouped[:]
+        )
+
+        def layer_norm(out, v, n):
+            stats = work.tile([P, 6], F32, name="stats")
+            nc.vector.bn_stats(out=stats[:], in_=v)
+            mean_var = work.tile([P, 2], F32, name="mean_var")
+            nc.vector.bn_aggr(out=mean_var[:], in_=stats[:])
+            mean = mean_var[:, 0:1]
+            var = mean_var[:, 1:2]
+            floor = work.tile([P, 1], F32, name="floor")
+            nc.vector.tensor_scalar(
+                out=floor[:], in0=var, scalar1=EPS, scalar2=VAR_FLOOR, op0=ALU.is_lt, op1=ALU.mult
+            )
+            spread2 = work.tile([P, 1], F32, name="spread2")
+            nc.vector.scalar_tensor_tensor(
+                out=spread2[:], in0=var, scalar=EPS, in1=floor[:], op0=ALU.add, op1=ALU.add
+            )
+            rstd = work.tile([P, 1], F32, name="rstd")
+            nc.gpsimd.tensor_tensor(out=rstd[:], in0=spread2[:], in1=minus_half[:], op=ALU.pow)
+            centred = work.tile([P, H], F32, name="centred")
+            nc.vector.scalar_tensor_tensor(
+                out=centred[:], in0=v, scalar=mean, in1=affine[n][:, 0:H],
+                op0=ALU.subtract, op1=ALU.mult,
+            )
+            nc.vector.scalar_tensor_tensor(
+                out=out, in0=centred[:], scalar=rstd[:], in1=affine[n][:, H : 2 * H],
+                op0=ALU.mult, op1=ALU.add,
+            )
+
+        def gate(g, func, bias):
+            acc = sums.tile([P, H], F32, name="acc")
+            w_codes = []
+            w_scales = []
+            for m in range(2):
+                grouped = staging.tile([P, 4 * H], BF16, align_bytes=64, name="w_grouped")
+                grouped_words = grouped[:].bitcast(F32)
+                rows_words = w_rows[(g, m)][:].bitcast(F32)
+                for half in range(2):
+                    bank = banks.tile([P, 512], F32, name="bank")
+                    planes = bank[:].rearrange("p (u c) -> p u c", u=2)
+                    for j in range(2):
+                        b = 2 * half + j
+                        transpose_words(planes, j * P, rows_words[:, b * WORDS : (b + 1) * WORDS])
+                    regroup(grouped_words[:, half * 512 : (half + 1) * 512], planes)
+                codes = operands.tile([P, H], U32, align_bytes=64, name="w_codes_%d_%d" % (g, m))
+                scales = operands.tile([P, H], U8, align_bytes=64, name="w_scales_%d_%d" % (g, m))
+                nc.vector.quantize_mx(out=codes[:].bitcast(FP8X4), scales=scales[:], in_=grouped[:])
+                w_codes.append(codes)
+                w_scales.append(scales)
+            for m in range(2):
+                nc.tensor.matmul_mx(
+                    out=acc[:],
+                    lhsT=act_codes[:, m * P : (m + 1) * P].bitcast(FP8X4),
+                    lhsT_scale=act_scales[:, m * P : (m + 1) * P],
+                    rhs=w_codes[m][:].bitcast(FP8X4),
+                    rhs_scale=w_scales[m][:],
+                    start=(m == 0),
+                    stop=(m == 1),
+                )
+            normed = work.tile([P, H], F32, name="normed")
+            layer_norm(normed[:], acc[:], g)
+            result = kept.tile([P, H], F32, name="gate_%d" % g)
+            if bias is None:
+                nc.scalar.activation(out=result[:], in_=normed[:], func=func)
+            else:
+                nc.scalar.activation(out=result[:], in_=normed[:], func=func, bias=bias)
+            return result
+
+        in_gate = gate(0, ACT.Sigmoid, None)
+        forget_gate = gate(1, ACT.Sigmoid, forget_bias[:])
+        cell = kept.tile([P, H], F32)
+        nc.vector.tensor_tensor(out=cell[:], in0=forget_gate[:], in1=cx_rows[:], op=ALU.mult)
+        cell_gate = gate(2, ACT.Tanh, None)
+        fresh = kept.tile([P, H], F32)
+        nc.vector.tensor_tensor(out=fresh[:], in0=in_gate[:], in1=cell_gate[:], op=ALU.mult)
+        nc.vector.tensor_tensor(out=cell[:], in0=cell[:], in1=fresh[:], op=ALU.add)
+        cy = kept.tile([P, H], F32)
+        layer_norm(cy[:], cell[:], 4)
+        nc.sync.dma_start(out=out_2[:, :], in_=cy[:])
+        tanh_cy = kept.tile([P, H], F32)
+        nc.scalar.activation(out=tanh_cy[:], in_=cy[:], func=ACT.Tanh)
+        out_gate = gate(3, ACT.Sigmoid, None)
+        hy = kept.tile([P, H], F32)
+        nc.vector.tensor_tensor(out=hy[:], in0=out_gate[:], in1=tanh_cy[:], op=ALU.mult)
+        nc.sync.dma_start(out=out_0[:, :], in_=hy[:])
+        nc.sync.dma_start(out=out_1[:, :], in_=hy[:])

@@ -14,14 +14,18 @@ ACT = mybir.ActivationFunctionType
 P = 128
 K = 512
 H = 512
+BANK = 512
 WORDS = K // 2
 ROW_BLOCKS = H // P
-NORMS = 5
+GATES = 4
+NORMS = GATES + 1
 EPS = 1e-12
 VAR_FLOOR = 0.01
 FORGET_BIAS = 1.0
+EARLY_NORMS = 3
+LATE_SPREAD_LAG = 3
 
-FLOPS = 2 * P * (4 * H) * (2 * K)
+FLOPS = 2 * P * (GATES * H) * (2 * K)
 
 
 def tile_layernormdropoutlstmcell_s_kernel(
@@ -29,175 +33,241 @@ def tile_layernormdropoutlstmcell_s_kernel(
 ):
     nc = tc.nc
     with ExitStack() as ctx:
+        ctx.enter_context(tc.manual_schedule())
         consts = ctx.enter_context(tc.tile_pool(name="consts", bufs=1))
         inputs = ctx.enter_context(tc.tile_pool(name="inputs", bufs=1))
-        staging = ctx.enter_context(tc.tile_pool(name="staging", bufs=3))
+        staging = ctx.enter_context(tc.tile_pool(name="staging", bufs=4))
         operands = ctx.enter_context(tc.tile_pool(name="operands", bufs=1))
         kept = ctx.enter_context(tc.tile_pool(name="kept", bufs=1))
-        work = ctx.enter_context(tc.tile_pool(name="work", bufs=2))
         banks = ctx.enter_context(tc.psum_pool(name="banks", bufs=4))
         sums = ctx.enter_context(tc.psum_pool(name="sums", bufs=4))
 
         affine_rows = consts.tile([P, H], BF16)
-        nc.vector.memset(affine_rows[:], 0.0)
-        minus_half = consts.tile([P, 1], F32)
-        nc.vector.memset(minus_half[:], -0.5)
-        forget_bias = consts.tile([P, 1], F32)
-        nc.vector.memset(forget_bias[:], FORGET_BIAS)
+        nc.gpsimd.memset(affine_rows[:], 0.0)
         ident = consts.tile([P, P], F32)
         make_identity(nc, ident[:])
+        minus_half = consts.tile([P, 1], F32)
+        nc.gpsimd.memset(minus_half[:], -0.5)
+        gate_bias = consts.tile([P, GATES], F32)
+        nc.gpsimd.memset(gate_bias[:], 0.0)
+        nc.gpsimd.memset(gate_bias[:, 1:2], FORGET_BIAS)
+        gate_func = (ACT.Sigmoid, ACT.Sigmoid, ACT.Tanh, ACT.Sigmoid)
 
-        nc.scalar.dma_start(out=affine_rows[0:NORMS, :], in_=gamma[:, :])
-        nc.scalar.dma_start(out=affine_rows[NORMS : 2 * NORMS, :], in_=beta[:, :])
-        cx_rows = inputs.tile([P, H], BF16)
-        nc.scalar.dma_start(out=cx_rows[:], in_=cx[:, :])
+        table_warm = consts.tile([P, 1], F32)
+        nc.scalar.activation(out=table_warm[:], in_=minus_half[:], func=ACT.Sigmoid)
+
         x_rows = inputs.tile([P, K], BF16)
         nc.sync.dma_start(out=x_rows[:], in_=x[:, :])
         hx_rows = inputs.tile([P, K], BF16)
         nc.sync.dma_start(out=hx_rows[:], in_=hx[:, :])
-        w_rows = {}
-        for g in range(4):
-            for m, weight in enumerate((weight_ih, weight_hh)):
-                rows = inputs.tile([P, ROW_BLOCKS * K], BF16, name="w_rows_%d_%d" % (g, m))
+        nc.sync.dma_start(out=affine_rows[0:NORMS, :], in_=gamma[:, :])
+        nc.sync.dma_start(out=affine_rows[NORMS : 2 * NORMS, :], in_=beta[:, :])
+        cx_rows = inputs.tile([P, H], BF16)
+        w_rows = []
+        for g in range(GATES):
+            for weight in (weight_ih, weight_hh):
+                rows = inputs.tile([P, ROW_BLOCKS * K], BF16, name="w_rows_%d" % len(w_rows))
                 nc.sync.dma_start(
                     out=rows[:].rearrange("p (b k) -> p b k", b=ROW_BLOCKS),
                     in_=weight[g * H : (g + 1) * H, :].rearrange("(b p) k -> p b k", p=P),
                 )
-                w_rows[(g, m)] = rows
+                w_rows.append(rows)
+            if g == 1:
+                nc.sync.dma_start(out=cx_rows[:], in_=cx[:, :])
 
-        table_warm = consts.tile([P, 1], F32)
-        nc.scalar.activation(out=table_warm[:], in_=forget_bias[:], func=ACT.Sigmoid)
+        def new_bank():
+            bank = banks.tile([P, BANK], F32, name="bank")
+            return bank
 
-        def transpose_words(bank_planes, column, rows_words):
+        def transpose_words(planes, column, rows_words):
             for u in range(2):
                 nc.tensor.transpose(
-                    bank_planes[:, u, column : column + P],
-                    rows_words[:, u * P : (u + 1) * P],
-                    ident[:],
+                    planes[:, u, column : column + P], rows_words[:, u * P : (u + 1) * P], ident[:]
                 )
 
-        def regroup(grouped_words, bank_planes):
+        def regroup(grouped_words, planes):
             nc.scalar.copy(
                 out=grouped_words.rearrange("p (c u) -> p c u", u=2),
-                in_=bank_planes.rearrange("p u c -> p c u"),
+                in_=planes.rearrange("p u c -> p c u"),
             )
 
-        bank = banks.tile([P, 512], F32, name="bank")
-        transpose_words(bank[:].rearrange("p (u c) -> p u c", u=2), 0, affine_rows[:].bitcast(F32))
-        affine_cols = consts.tile([P, 2, 2 * NORMS], F32)
-        nc.vector.tensor_copy(
-            out=affine_cols[:],
-            in_=bank[:].rearrange("p (u c) -> p u c", u=2)[:, :, 0 : 2 * NORMS],
-        )
-        affine = []
-        for n in range(NORMS):
-            bank = banks.tile([P, 512], F32, name="bank")
-            for s in range(2):
-                for u in range(2):
-                    column = (2 * s + u) * P
-                    row = s * NORMS + n
-                    nc.tensor.transpose(
-                        bank[:, column : column + P],
-                        affine_cols[:, u, row : row + 1].to_broadcast([P, P]),
-                        ident[:],
-                    )
-            spread = consts.tile([P, 2 * H], BF16, name="affine_%d" % n)
-            nc.scalar.copy(out=spread[:].bitcast(F32), in_=bank[:])
-            affine.append(spread)
-
-        bank = banks.tile([P, 512], F32, name="bank")
+        bank = new_bank()
         planes = bank[:].rearrange("p (u c) -> p u c", u=2)
         transpose_words(planes, 0, x_rows[:].bitcast(F32))
         transpose_words(planes, P, hx_rows[:].bitcast(F32))
         act_grouped = staging.tile([P, 4 * 2 * P], BF16, align_bytes=64)
         regroup(act_grouped[:].bitcast(F32), planes)
+
+        bank = new_bank()
+        planes = bank[:].rearrange("p (u c) -> p u c", u=2)
+        transpose_words(planes, 0, affine_rows[:].bitcast(F32))
+        affine_cols = consts.tile([P, 2, 2 * NORMS], F32)
+        nc.vector.tensor_copy(out=affine_cols[:], in_=planes[:, :, 0 : 2 * NORMS])
+
         act_codes = operands.tile([P, 2 * P], U32, align_bytes=64)
         act_scales = operands.tile([P, 2 * P], U8, align_bytes=64)
         nc.vector.quantize_mx(
             out=act_codes[:].bitcast(FP8X4), scales=act_scales[:], in_=act_grouped[:]
         )
 
-        def layer_norm(out, v, n):
-            stats = work.tile([P, 6], F32, name="stats")
-            nc.vector.bn_stats(out=stats[:], in_=v)
-            mean_var = work.tile([P, 2], F32, name="mean_var")
-            nc.vector.bn_aggr(out=mean_var[:], in_=stats[:])
-            mean = mean_var[:, 0:1]
-            var = mean_var[:, 1:2]
-            floor = work.tile([P, 1], F32, name="floor")
-            nc.vector.tensor_scalar(
+        spread_bank = {}
+        affine = {}
+
+        def spread_transposes(n):
+            spread_bank[n] = new_bank()
+            for s in range(2):
+                for u in range(2):
+                    column = (2 * s + u) * P
+                    row = s * NORMS + n
+                    nc.tensor.transpose(
+                        spread_bank[n][:, column : column + P],
+                        affine_cols[:, u, row : row + 1].to_broadcast([P, P]),
+                        ident[:],
+                    )
+
+        def spread_copy(n, copy):
+            affine[n] = consts.tile([P, 2 * H], BF16, name="affine_%d" % n)
+            copy(out=affine[n][:].bitcast(F32), in_=spread_bank[n][:])
+
+        grouped = {}
+        w_codes = {}
+        w_scales = {}
+
+        def unit_to_k_major(u):
+            grouped[u] = staging.tile([P, 4 * H], BF16, align_bytes=64, name="w_grouped")
+            grouped_words = grouped[u][:].bitcast(F32)
+            rows_words = w_rows[u][:].bitcast(F32)
+            for half in range(2):
+                bank = new_bank()
+                planes = bank[:].rearrange("p (u c) -> p u c", u=2)
+                for j in range(2):
+                    b = 2 * half + j
+                    transpose_words(planes, j * P, rows_words[:, b * WORDS : (b + 1) * WORDS])
+                regroup(grouped_words[:, half * BANK : (half + 1) * BANK], planes)
+
+        def quantise(u):
+            w_codes[u] = operands.tile([P, H], U32, align_bytes=64, name="w_codes_%d" % u)
+            w_scales[u] = operands.tile([P, H], U8, align_bytes=64, name="w_scales_%d" % u)
+            nc.vector.quantize_mx(
+                out=w_codes[u][:].bitcast(FP8X4), scales=w_scales[u][:], in_=grouped[u][:]
+            )
+
+        acc = {}
+
+        def mx_pass(u):
+            g, m = divmod(u, 2)
+            if m == 0:
+                acc[g] = sums.tile([P, H], F32, name="acc")
+            nc.tensor.matmul_mx(
+                out=acc[g][:],
+                lhsT=act_codes[:, m * P : (m + 1) * P].bitcast(FP8X4),
+                lhsT_scale=act_scales[:, m * P : (m + 1) * P],
+                rhs=w_codes[u][:].bitcast(FP8X4),
+                rhs_scale=w_scales[u][:],
+                start=(m == 0),
+                stop=(m == 1),
+            )
+
+        stats = {}
+        mean_var = {}
+        rstd = {}
+        centred = {}
+
+        def norm_stats(n, v):
+            stats[n] = kept.tile([P, 6], F32, name="stats_%d" % n)
+            nc.vector.bn_stats(out=stats[n][:], in_=v)
+
+        def norm_moments(n):
+            mean_var[n] = kept.tile([P, 2], F32, name="mean_var_%d" % n)
+            nc.vector.bn_aggr(out=mean_var[n][:], in_=stats[n][:])
+            var = mean_var[n][:, 1:2]
+            floor = kept.tile([P, 1], F32, name="floor_%d" % n)
+            nc.gpsimd.tensor_scalar(
                 out=floor[:], in0=var, scalar1=EPS, scalar2=VAR_FLOOR, op0=ALU.is_lt, op1=ALU.mult
             )
-            spread2 = work.tile([P, 1], F32, name="spread2")
-            nc.vector.scalar_tensor_tensor(
-                out=spread2[:], in0=var, scalar=EPS, in1=floor[:], op0=ALU.add, op1=ALU.add
+            padded = kept.tile([P, 1], F32, name="padded_%d" % n)
+            nc.gpsimd.tensor_scalar(
+                out=padded[:], in0=floor[:], scalar1=var, scalar2=EPS, op0=ALU.add, op1=ALU.add
             )
-            rstd = work.tile([P, 1], F32, name="rstd")
-            nc.gpsimd.tensor_tensor(out=rstd[:], in0=spread2[:], in1=minus_half[:], op=ALU.pow)
-            centred = work.tile([P, H], F32, name="centred")
+            rstd[n] = kept.tile([P, 1], F32, name="rstd_%d" % n)
+            nc.gpsimd.tensor_tensor(out=rstd[n][:], in0=padded[:], in1=minus_half[:], op=ALU.pow)
+
+        def norm_centre(n, v):
+            centred[n] = kept.tile([P, H], F32, name="centred_%d" % n)
             nc.vector.scalar_tensor_tensor(
-                out=centred[:], in0=v, scalar=mean, in1=affine[n][:, 0:H],
+                out=centred[n][:], in0=v, scalar=mean_var[n][:, 0:1], in1=affine[n][:, 0:H],
                 op0=ALU.subtract, op1=ALU.mult,
             )
+
+        def norm_finish(n, out):
             nc.vector.scalar_tensor_tensor(
-                out=out, in0=centred[:], scalar=rstd[:], in1=affine[n][:, H : 2 * H],
+                out=out, in0=centred[n][:], scalar=rstd[n][:], in1=affine[n][:, H : 2 * H],
                 op0=ALU.mult, op1=ALU.add,
             )
 
-        def gate(g, func, bias):
-            acc = sums.tile([P, H], F32, name="acc")
-            w_codes = []
-            w_scales = []
-            for m in range(2):
-                grouped = staging.tile([P, 4 * H], BF16, align_bytes=64, name="w_grouped")
-                grouped_words = grouped[:].bitcast(F32)
-                rows_words = w_rows[(g, m)][:].bitcast(F32)
-                for half in range(2):
-                    bank = banks.tile([P, 512], F32, name="bank")
-                    planes = bank[:].rearrange("p (u c) -> p u c", u=2)
-                    for j in range(2):
-                        b = 2 * half + j
-                        transpose_words(planes, j * P, rows_words[:, b * WORDS : (b + 1) * WORDS])
-                    regroup(grouped_words[:, half * 512 : (half + 1) * 512], planes)
-                codes = operands.tile([P, H], U32, align_bytes=64, name="w_codes_%d_%d" % (g, m))
-                scales = operands.tile([P, H], U8, align_bytes=64, name="w_scales_%d_%d" % (g, m))
-                nc.vector.quantize_mx(out=codes[:].bitcast(FP8X4), scales=scales[:], in_=grouped[:])
-                w_codes.append(codes)
-                w_scales.append(scales)
-            for m in range(2):
-                nc.tensor.matmul_mx(
-                    out=acc[:],
-                    lhsT=act_codes[:, m * P : (m + 1) * P].bitcast(FP8X4),
-                    lhsT_scale=act_scales[:, m * P : (m + 1) * P],
-                    rhs=w_codes[m][:].bitcast(FP8X4),
-                    rhs_scale=w_scales[m][:],
-                    start=(m == 0),
-                    stop=(m == 1),
-                )
-            normed = work.tile([P, H], F32, name="normed")
-            layer_norm(normed[:], acc[:], g)
-            result = kept.tile([P, H], F32, name="gate_%d" % g)
-            if bias is None:
-                nc.scalar.activation(out=result[:], in_=normed[:], func=func)
-            else:
-                nc.scalar.activation(out=result[:], in_=normed[:], func=func, bias=bias)
-            return result
+        normed = {}
+        gate = {}
 
-        in_gate = gate(0, ACT.Sigmoid, None)
-        forget_gate = gate(1, ACT.Sigmoid, forget_bias[:])
-        cell = kept.tile([P, H], F32)
-        nc.vector.tensor_tensor(out=cell[:], in0=forget_gate[:], in1=cx_rows[:], op=ALU.mult)
-        cell_gate = gate(2, ACT.Tanh, None)
+        def apply_function(g):
+            gate[g] = kept.tile([P, H], F32, name="gate_%d" % g)
+            nc.scalar.activation(
+                out=gate[g][:], in_=normed[g][:], func=gate_func[g], bias=gate_bias[:, g : g + 1]
+            )
+
+        def finish_gate_norm(g):
+            normed[g] = kept.tile([P, H], F32, name="normed_%d" % g)
+            norm_finish(g, normed[g][:])
+
+        for n in range(EARLY_NORMS):
+            spread_transposes(n)
+        for n in range(EARLY_NORMS):
+            spread_copy(n, nc.vector.tensor_copy)
+
+        for j in range(GATES):
+            for u in (2 * j, 2 * j + 1):
+                unit_to_k_major(u)
+                if u >= 2:
+                    mx_pass(u - 2)
+                if u - LATE_SPREAD_LAG >= EARLY_NORMS:
+                    spread_transposes(u - LATE_SPREAD_LAG)
+                    spread_copy(u - LATE_SPREAD_LAG, nc.scalar.copy)
+            quantise(2 * j)
+            if j >= 1:
+                norm_stats(j - 1, acc[j - 1][:])
+            quantise(2 * j + 1)
+            if j >= 1:
+                norm_moments(j - 1)
+            if j >= 2:
+                finish_gate_norm(j - 2)
+            if j >= 1:
+                norm_centre(j - 1, acc[j - 1][:])
+        mx_pass(2 * GATES - 2)
+        mx_pass(2 * GATES - 1)
+        apply_function(0)
+        apply_function(1)
+
+        held = kept.tile([P, H], F32)
+        nc.vector.tensor_tensor(out=held[:], in0=gate[1][:], in1=cx_rows[:], op=ALU.mult)
+        finish_gate_norm(2)
+        apply_function(2)
+        norm_stats(3, acc[3][:])
+        norm_moments(3)
         fresh = kept.tile([P, H], F32)
-        nc.vector.tensor_tensor(out=fresh[:], in0=in_gate[:], in1=cell_gate[:], op=ALU.mult)
-        nc.vector.tensor_tensor(out=cell[:], in0=cell[:], in1=fresh[:], op=ALU.add)
+        nc.vector.tensor_tensor(out=fresh[:], in0=gate[0][:], in1=gate[2][:], op=ALU.mult)
+        cell = kept.tile([P, H], F32)
+        nc.vector.tensor_tensor(out=cell[:], in0=held[:], in1=fresh[:], op=ALU.add)
+        norm_stats(GATES, cell[:])
+        norm_centre(3, acc[3][:])
+        norm_moments(GATES)
+        norm_centre(GATES, cell[:])
+        finish_gate_norm(3)
+        apply_function(3)
         cy = kept.tile([P, H], F32)
-        layer_norm(cy[:], cell[:], 4)
+        norm_finish(GATES, cy[:])
         nc.sync.dma_start(out=out_2[:, :], in_=cy[:])
         tanh_cy = kept.tile([P, H], F32)
         nc.scalar.activation(out=tanh_cy[:], in_=cy[:], func=ACT.Tanh)
-        out_gate = gate(3, ACT.Sigmoid, None)
         hy = kept.tile([P, H], F32)
-        nc.vector.tensor_tensor(out=hy[:], in0=out_gate[:], in1=tanh_cy[:], op=ALU.mult)
+        nc.vector.tensor_tensor(out=hy[:], in0=gate[3][:], in1=tanh_cy[:], op=ALU.mult)
         nc.sync.dma_start(out=out_0[:, :], in_=hy[:])
         nc.sync.dma_start(out=out_1[:, :], in_=hy[:])

@@ -7,6 +7,7 @@ F32 = mybir.dt.float32
 BF16 = mybir.dt.bfloat16
 U32 = mybir.dt.uint32
 U8 = mybir.dt.uint8
+I32 = mybir.dt.int32
 FP8X4 = mybir.dt.float8_e4m3fn_x4
 ALU = mybir.AluOpType
 ACT = mybir.ActivationFunctionType
@@ -23,6 +24,7 @@ EPS = 1e-12
 VAR_FLOOR = 0.01
 FORGET_BIAS = 1.0
 EARLY_NORMS = 3
+KICK = 4
 LATE_SPREAD_LAG = 3
 
 FLOPS = 2 * P * (GATES * H) * (2 * K)
@@ -40,7 +42,31 @@ def tile_layernormdropoutlstmcell_s_kernel(
         operands = ctx.enter_context(tc.tile_pool(name="operands", bufs=1))
         kept = ctx.enter_context(tc.tile_pool(name="kept", bufs=1))
         banks = ctx.enter_context(tc.psum_pool(name="banks", bufs=4))
-        sums = ctx.enter_context(tc.psum_pool(name="sums", bufs=4))
+        sums = ctx.enter_context(tc.psum_pool(name="sums", bufs=3))
+        spare = ctx.enter_context(tc.psum_pool(name="spare", bufs=1))
+
+        zeros = consts.tile([P, 4 * H], BF16, align_bytes=64)
+        nc.vector.memset(zeros[:].bitcast(I32), 0)
+        zero_codes = consts.tile([P, H], U32, align_bytes=64)
+        zero_scales = consts.tile([P, H], U8, align_bytes=64)
+        nc.vector.quantize_mx(
+            out=zero_codes[:].bitcast(FP8X4), scales=zero_scales[:], in_=zeros[:]
+        )
+        unread = spare.tile([P, H], F32)
+
+        def keep_warm(passes):
+            for i in range(passes):
+                nc.tensor.matmul_mx(
+                    out=unread[:],
+                    lhsT=zero_codes[:, 0:P].bitcast(FP8X4),
+                    lhsT_scale=zero_scales[:, 0:P],
+                    rhs=zero_codes[:].bitcast(FP8X4),
+                    rhs_scale=zero_scales[:],
+                    start=(i == 0),
+                    stop=(i == passes - 1),
+                )
+
+        keep_warm(KICK)
 
         affine_rows = consts.tile([P, H], BF16)
         nc.gpsimd.memset(affine_rows[:], 0.0)
@@ -220,6 +246,7 @@ def tile_layernormdropoutlstmcell_s_kernel(
 
         for n in range(EARLY_NORMS):
             spread_transposes(n)
+        keep_warm(2)
         for n in range(EARLY_NORMS):
             spread_copy(n, nc.vector.tensor_copy)
 
@@ -228,6 +255,9 @@ def tile_layernormdropoutlstmcell_s_kernel(
                 unit_to_k_major(u)
                 if u >= 2:
                     mx_pass(u - 2)
+                    keep_warm(1)
+                else:
+                    keep_warm(2)
                 if u - LATE_SPREAD_LAG >= EARLY_NORMS:
                     spread_transposes(u - LATE_SPREAD_LAG)
                     spread_copy(u - LATE_SPREAD_LAG, nc.scalar.copy)

@@ -5,9 +5,9 @@ from concourse.masks import make_identity
 
 F32 = mybir.dt.float32
 BF16 = mybir.dt.bfloat16
+I32 = mybir.dt.int32
 U32 = mybir.dt.uint32
 U8 = mybir.dt.uint8
-I32 = mybir.dt.int32
 FP8X4 = mybir.dt.float8_e4m3fn_x4
 ALU = mybir.AluOpType
 ACT = mybir.ActivationFunctionType
@@ -19,13 +19,15 @@ BANK = 512
 WORDS = K // 2
 ROW_BLOCKS = H // P
 GATES = 4
+I_GATE = 0
+F_GATE = 1
+G_GATE = 2
+O_GATE = 3
+CELL = GATES
 NORMS = GATES + 1
 EPS = 1e-12
 VAR_FLOOR = 0.01
 FORGET_BIAS = 1.0
-EARLY_NORMS = 3
-KICK = 4
-LATE_SPREAD_LAG = 3
 
 FLOPS = 2 * P * (GATES * H) * (2 * K)
 
@@ -42,41 +44,17 @@ def tile_layernormdropoutlstmcell_s_kernel(
         operands = ctx.enter_context(tc.tile_pool(name="operands", bufs=1))
         kept = ctx.enter_context(tc.tile_pool(name="kept", bufs=1))
         banks = ctx.enter_context(tc.psum_pool(name="banks", bufs=4))
-        sums = ctx.enter_context(tc.psum_pool(name="sums", bufs=3))
-        spare = ctx.enter_context(tc.psum_pool(name="spare", bufs=1))
-
-        zeros = consts.tile([P, 4 * H], BF16, align_bytes=64)
-        nc.vector.memset(zeros[:].bitcast(I32), 0)
-        zero_codes = consts.tile([P, H], U32, align_bytes=64)
-        zero_scales = consts.tile([P, H], U8, align_bytes=64)
-        nc.vector.quantize_mx(
-            out=zero_codes[:].bitcast(FP8X4), scales=zero_scales[:], in_=zeros[:]
-        )
-        unread = spare.tile([P, H], F32)
-
-        def keep_warm(passes):
-            for i in range(passes):
-                nc.tensor.matmul_mx(
-                    out=unread[:],
-                    lhsT=zero_codes[:, 0:P].bitcast(FP8X4),
-                    lhsT_scale=zero_scales[:, 0:P],
-                    rhs=zero_codes[:].bitcast(FP8X4),
-                    rhs_scale=zero_scales[:],
-                    start=(i == 0),
-                    stop=(i == passes - 1),
-                )
-
-        keep_warm(KICK)
+        sums = ctx.enter_context(tc.psum_pool(name="sums", bufs=4))
 
         affine_rows = consts.tile([P, H], BF16)
-        nc.gpsimd.memset(affine_rows[:], 0.0)
+        nc.vector.memset(affine_rows[:].bitcast(I32), 0)
         ident = consts.tile([P, P], F32)
         make_identity(nc, ident[:])
         minus_half = consts.tile([P, 1], F32)
         nc.gpsimd.memset(minus_half[:], -0.5)
         gate_bias = consts.tile([P, GATES], F32)
         nc.gpsimd.memset(gate_bias[:], 0.0)
-        nc.gpsimd.memset(gate_bias[:, 1:2], FORGET_BIAS)
+        nc.gpsimd.memset(gate_bias[:, F_GATE : F_GATE + 1], FORGET_BIAS)
         gate_func = (ACT.Sigmoid, ACT.Sigmoid, ACT.Tanh, ACT.Sigmoid)
 
         table_warm = consts.tile([P, 1], F32)
@@ -84,13 +62,15 @@ def tile_layernormdropoutlstmcell_s_kernel(
 
         x_rows = inputs.tile([P, K], BF16)
         nc.sync.dma_start(out=x_rows[:], in_=x[:, :])
-        hx_rows = inputs.tile([P, K], BF16)
-        nc.sync.dma_start(out=hx_rows[:], in_=hx[:, :])
         nc.sync.dma_start(out=affine_rows[0:NORMS, :], in_=gamma[:, :])
         nc.sync.dma_start(out=affine_rows[NORMS : 2 * NORMS, :], in_=beta[:, :])
+        hx_rows = inputs.tile([P, K], BF16)
+        nc.sync.dma_start(out=hx_rows[:], in_=hx[:, :])
         cx_rows = inputs.tile([P, H], BF16)
         w_rows = []
         for g in range(GATES):
+            if g == O_GATE:
+                nc.sync.dma_start(out=cx_rows[:], in_=cx[:, :])
             for weight in (weight_ih, weight_hh):
                 rows = inputs.tile([P, ROW_BLOCKS * K], BF16, name="w_rows_%d" % len(w_rows))
                 nc.sync.dma_start(
@@ -98,8 +78,6 @@ def tile_layernormdropoutlstmcell_s_kernel(
                     in_=weight[g * H : (g + 1) * H, :].rearrange("(b p) k -> p b k", p=P),
                 )
                 w_rows.append(rows)
-            if g == 1:
-                nc.sync.dma_start(out=cx_rows[:], in_=cx[:, :])
 
         def new_bank():
             bank = banks.tile([P, BANK], F32, name="bank")
@@ -116,25 +94,6 @@ def tile_layernormdropoutlstmcell_s_kernel(
                 out=grouped_words.rearrange("p (c u) -> p c u", u=2),
                 in_=planes.rearrange("p u c -> p c u"),
             )
-
-        bank = new_bank()
-        planes = bank[:].rearrange("p (u c) -> p u c", u=2)
-        transpose_words(planes, 0, x_rows[:].bitcast(F32))
-        transpose_words(planes, P, hx_rows[:].bitcast(F32))
-        act_grouped = staging.tile([P, 4 * 2 * P], BF16, align_bytes=64)
-        regroup(act_grouped[:].bitcast(F32), planes)
-
-        bank = new_bank()
-        planes = bank[:].rearrange("p (u c) -> p u c", u=2)
-        transpose_words(planes, 0, affine_rows[:].bitcast(F32))
-        affine_cols = consts.tile([P, 2, 2 * NORMS], F32)
-        nc.vector.tensor_copy(out=affine_cols[:], in_=planes[:, :, 0 : 2 * NORMS])
-
-        act_codes = operands.tile([P, 2 * P], U32, align_bytes=64)
-        act_scales = operands.tile([P, 2 * P], U8, align_bytes=64)
-        nc.vector.quantize_mx(
-            out=act_codes[:].bitcast(FP8X4), scales=act_scales[:], in_=act_grouped[:]
-        )
 
         spread_bank = {}
         affine = {}
@@ -225,13 +184,16 @@ def tile_layernormdropoutlstmcell_s_kernel(
                 op0=ALU.subtract, op1=ALU.mult,
             )
 
-        def norm_finish(n, out):
+        normed = {}
+
+        def norm_finish(n, cols):
+            if n not in normed:
+                normed[n] = kept.tile([P, H], F32, name="normed_%d" % n)
             nc.vector.scalar_tensor_tensor(
-                out=out, in0=centred[n][:], scalar=rstd[n][:], in1=affine[n][:, H : 2 * H],
-                op0=ALU.mult, op1=ALU.add,
+                out=normed[n][:, cols], in0=centred[n][:, cols], scalar=rstd[n][:],
+                in1=affine[n][:, H : 2 * H][:, cols], op0=ALU.mult, op1=ALU.add,
             )
 
-        normed = {}
         gate = {}
 
         def apply_function(g):
@@ -240,27 +202,37 @@ def tile_layernormdropoutlstmcell_s_kernel(
                 out=gate[g][:], in_=normed[g][:], func=gate_func[g], bias=gate_bias[:, g : g + 1]
             )
 
-        def finish_gate_norm(g):
-            normed[g] = kept.tile([P, H], F32, name="normed_%d" % g)
-            norm_finish(g, normed[g][:])
+        whole = slice(0, H)
+        halves = (slice(0, H // 2), slice(H // 2, H))
 
-        for n in range(EARLY_NORMS):
+        bank = new_bank()
+        planes = bank[:].rearrange("p (u c) -> p u c", u=2)
+        transpose_words(planes, 0, affine_rows[:].bitcast(F32))
+        affine_cols = consts.tile([P, 2, 2 * NORMS], F32)
+        nc.vector.tensor_copy(out=affine_cols[:], in_=planes[:, :, 0 : 2 * NORMS])
+
+        bank = new_bank()
+        planes = bank[:].rearrange("p (u c) -> p u c", u=2)
+        transpose_words(planes, 0, x_rows[:].bitcast(F32))
+        transpose_words(planes, P, hx_rows[:].bitcast(F32))
+        act_grouped = staging.tile([P, 4 * 2 * P], BF16, align_bytes=64)
+        regroup(act_grouped[:].bitcast(F32), planes)
+        act_codes = operands.tile([P, 2 * P], U32, align_bytes=64)
+        act_scales = operands.tile([P, 2 * P], U8, align_bytes=64)
+        nc.vector.quantize_mx(
+            out=act_codes[:].bitcast(FP8X4), scales=act_scales[:], in_=act_grouped[:]
+        )
+
+        for n in (I_GATE, F_GATE, G_GATE):
             spread_transposes(n)
-        keep_warm(2)
-        for n in range(EARLY_NORMS):
+        for n in (I_GATE, F_GATE, G_GATE):
             spread_copy(n, nc.vector.tensor_copy)
 
-        for j in range(GATES):
+        for j in (I_GATE, F_GATE, G_GATE):
             for u in (2 * j, 2 * j + 1):
                 unit_to_k_major(u)
                 if u >= 2:
                     mx_pass(u - 2)
-                    keep_warm(1)
-                else:
-                    keep_warm(2)
-                if u - LATE_SPREAD_LAG >= EARLY_NORMS:
-                    spread_transposes(u - LATE_SPREAD_LAG)
-                    spread_copy(u - LATE_SPREAD_LAG, nc.scalar.copy)
             quantise(2 * j)
             if j >= 1:
                 norm_stats(j - 1, acc[j - 1][:])
@@ -268,36 +240,55 @@ def tile_layernormdropoutlstmcell_s_kernel(
             if j >= 1:
                 norm_moments(j - 1)
             if j >= 2:
-                finish_gate_norm(j - 2)
+                norm_finish(j - 2, whole)
             if j >= 1:
                 norm_centre(j - 1, acc[j - 1][:])
-        mx_pass(2 * GATES - 2)
-        mx_pass(2 * GATES - 1)
-        apply_function(0)
-        apply_function(1)
 
+        unit_to_k_major(2 * O_GATE)
+        mx_pass(2 * G_GATE)
+        mx_pass(2 * G_GATE + 1)
+        unit_to_k_major(2 * O_GATE + 1)
+        for n in (O_GATE, CELL):
+            spread_transposes(n)
+            spread_copy(n, nc.scalar.copy)
+
+        norm_stats(G_GATE, acc[G_GATE][:])
+        quantise(2 * O_GATE)
+        norm_moments(G_GATE)
+        quantise(2 * O_GATE + 1)
+        norm_centre(G_GATE, acc[G_GATE][:])
+        norm_finish(F_GATE, whole)
+        norm_finish(G_GATE, whole)
+        mx_pass(2 * O_GATE)
+        mx_pass(2 * O_GATE + 1)
+        for g in (I_GATE, F_GATE, G_GATE):
+            apply_function(g)
+
+        norm_stats(O_GATE, acc[O_GATE][:])
         held = kept.tile([P, H], F32)
-        nc.vector.tensor_tensor(out=held[:], in0=gate[1][:], in1=cx_rows[:], op=ALU.mult)
-        finish_gate_norm(2)
-        apply_function(2)
-        norm_stats(3, acc[3][:])
-        norm_moments(3)
+        nc.vector.tensor_tensor(out=held[:], in0=gate[F_GATE][:], in1=cx_rows[:], op=ALU.mult)
         fresh = kept.tile([P, H], F32)
-        nc.vector.tensor_tensor(out=fresh[:], in0=gate[0][:], in1=gate[2][:], op=ALU.mult)
+        nc.vector.tensor_tensor(out=fresh[:], in0=gate[I_GATE][:], in1=gate[G_GATE][:], op=ALU.mult)
+        norm_moments(O_GATE)
         cell = kept.tile([P, H], F32)
         nc.vector.tensor_tensor(out=cell[:], in0=held[:], in1=fresh[:], op=ALU.add)
-        norm_stats(GATES, cell[:])
-        norm_centre(3, acc[3][:])
-        norm_moments(GATES)
-        norm_centre(GATES, cell[:])
-        finish_gate_norm(3)
-        apply_function(3)
-        cy = kept.tile([P, H], F32)
-        norm_finish(GATES, cy[:])
-        nc.sync.dma_start(out=out_2[:, :], in_=cy[:])
+        norm_stats(CELL, cell[:])
+        norm_moments(CELL)
+        norm_centre(O_GATE, acc[O_GATE][:])
+        norm_centre(CELL, cell[:])
+        norm_finish(O_GATE, whole)
+        apply_function(O_GATE)
+
         tanh_cy = kept.tile([P, H], F32)
-        nc.scalar.activation(out=tanh_cy[:], in_=cy[:], func=ACT.Tanh)
         hy = kept.tile([P, H], F32)
-        nc.vector.tensor_tensor(out=hy[:], in0=gate[3][:], in1=tanh_cy[:], op=ALU.mult)
-        nc.sync.dma_start(out=out_0[:, :], in_=hy[:])
-        nc.sync.dma_start(out=out_1[:, :], in_=hy[:])
+        for cols in halves:
+            norm_finish(CELL, cols)
+        nc.sync.dma_start(out=out_2[:, :], in_=normed[CELL][:])
+        for cols in halves:
+            nc.scalar.activation(out=tanh_cy[:, cols], in_=normed[CELL][:, cols], func=ACT.Tanh)
+        for cols in halves:
+            nc.vector.tensor_tensor(
+                out=hy[:, cols], in0=gate[O_GATE][:, cols], in1=tanh_cy[:, cols], op=ALU.mult
+            )
+            nc.sync.dma_start(out=out_0[:, cols], in_=hy[:, cols])
+            nc.sync.dma_start(out=out_1[:, cols], in_=hy[:, cols])

from contextlib import ExitStack

import concourse.mybir as mybir
from concourse.masks import make_identity

F32 = mybir.dt.float32
BF16 = mybir.dt.bfloat16
I32 = mybir.dt.int32
U32 = mybir.dt.uint32
U8 = mybir.dt.uint8
FP8X4 = mybir.dt.float8_e4m3fn_x4
ALU = mybir.AluOpType
ACT = mybir.ActivationFunctionType

P = 128
K = 512
H = 512
BANK = 512
WORDS = K // 2
ROW_BLOCKS = H // P
GATES = 4
I_GATE = 0
F_GATE = 1
G_GATE = 2
O_GATE = 3
CELL = GATES
NORMS = GATES + 1
EPS = 1e-12
VAR_FLOOR = 0.01
FORGET_BIAS = 1.0

FLOPS = 2 * P * (GATES * H) * (2 * K)


def tile_layernormdropoutlstmcell_s_kernel(
    tc, x, hx, cx, weight_ih, weight_hh, gamma, beta, out_0, out_1, out_2
):
    nc = tc.nc
    with ExitStack() as ctx:
        ctx.enter_context(tc.manual_schedule())
        consts = ctx.enter_context(tc.tile_pool(name="consts", bufs=1))
        inputs = ctx.enter_context(tc.tile_pool(name="inputs", bufs=1))
        staging = ctx.enter_context(tc.tile_pool(name="staging", bufs=4))
        operands = ctx.enter_context(tc.tile_pool(name="operands", bufs=1))
        kept = ctx.enter_context(tc.tile_pool(name="kept", bufs=1))
        banks = ctx.enter_context(tc.psum_pool(name="banks", bufs=4))
        sums = ctx.enter_context(tc.psum_pool(name="sums", bufs=4))

        affine_rows = consts.tile([P, H], BF16)
        nc.vector.memset(affine_rows[:].bitcast(I32), 0)
        ident = consts.tile([P, P], F32)
        make_identity(nc, ident[:])
        minus_half = consts.tile([P, 1], F32)
        nc.gpsimd.memset(minus_half[:], -0.5)
        gate_bias = consts.tile([P, GATES], F32)
        nc.gpsimd.memset(gate_bias[:], 0.0)
        nc.gpsimd.memset(gate_bias[:, F_GATE : F_GATE + 1], FORGET_BIAS)
        gate_func = (ACT.Sigmoid, ACT.Sigmoid, ACT.Tanh, ACT.Sigmoid)

        table_warm = consts.tile([P, 1], F32)
        nc.scalar.activation(out=table_warm[:], in_=minus_half[:], func=ACT.Sigmoid)

        x_rows = inputs.tile([P, K], BF16)
        nc.sync.dma_start(out=x_rows[:], in_=x[:, :])
        nc.sync.dma_start(out=affine_rows[0:NORMS, :], in_=gamma[:, :])
        nc.sync.dma_start(out=affine_rows[NORMS : 2 * NORMS, :], in_=beta[:, :])
        hx_rows = inputs.tile([P, K], BF16)
        nc.sync.dma_start(out=hx_rows[:], in_=hx[:, :])
        cx_rows = inputs.tile([P, H], BF16)
        w_rows = []
        for g in range(GATES):
            if g == O_GATE:
                nc.sync.dma_start(out=cx_rows[:], in_=cx[:, :])
            for weight in (weight_ih, weight_hh):
                rows = inputs.tile([P, ROW_BLOCKS * K], BF16, name="w_rows_%d" % len(w_rows))
                nc.sync.dma_start(
                    out=rows[:].rearrange("p (b k) -> p b k", b=ROW_BLOCKS),
                    in_=weight[g * H : (g + 1) * H, :].rearrange("(b p) k -> p b k", p=P),
                )
                w_rows.append(rows)

        def new_bank():
            bank = banks.tile([P, BANK], F32, name="bank")
            return bank

        def transpose_words(planes, column, rows_words):
            for u in range(2):
                nc.tensor.transpose(
                    planes[:, u, column : column + P], rows_words[:, u * P : (u + 1) * P], ident[:]
                )

        def regroup(grouped_words, planes):
            nc.scalar.copy(
                out=grouped_words.rearrange("p (c u) -> p c u", u=2),
                in_=planes.rearrange("p u c -> p c u"),
            )

        spread_bank = {}
        affine = {}

        def spread_transposes(n):
            spread_bank[n] = new_bank()
            for s in range(2):
                for u in range(2):
                    column = (2 * s + u) * P
                    row = s * NORMS + n
                    nc.tensor.transpose(
                        spread_bank[n][:, column : column + P],
                        affine_cols[:, u, row : row + 1].to_broadcast([P, P]),
                        ident[:],
                    )

        def spread_copy(n, copy):
            affine[n] = consts.tile([P, 2 * H], BF16, name="affine_%d" % n)
            copy(out=affine[n][:].bitcast(F32), in_=spread_bank[n][:])

        grouped = {}
        w_codes = {}
        w_scales = {}

        def unit_to_k_major(u):
            grouped[u] = staging.tile([P, 4 * H], BF16, align_bytes=64, name="w_grouped")
            grouped_words = grouped[u][:].bitcast(F32)
            rows_words = w_rows[u][:].bitcast(F32)
            for half in range(2):
                bank = new_bank()
                planes = bank[:].rearrange("p (u c) -> p u c", u=2)
                for j in range(2):
                    b = 2 * half + j
                    transpose_words(planes, j * P, rows_words[:, b * WORDS : (b + 1) * WORDS])
                regroup(grouped_words[:, half * BANK : (half + 1) * BANK], planes)

        def quantise(u):
            w_codes[u] = operands.tile([P, H], U32, align_bytes=64, name="w_codes_%d" % u)
            w_scales[u] = operands.tile([P, H], U8, align_bytes=64, name="w_scales_%d" % u)
            nc.vector.quantize_mx(
                out=w_codes[u][:].bitcast(FP8X4), scales=w_scales[u][:], in_=grouped[u][:]
            )

        acc = {}

        def mx_pass(u):
            g, m = divmod(u, 2)
            if m == 0:
                acc[g] = sums.tile([P, H], F32, name="acc")
            nc.tensor.matmul_mx(
                out=acc[g][:],
                lhsT=act_codes[:, m * P : (m + 1) * P].bitcast(FP8X4),
                lhsT_scale=act_scales[:, m * P : (m + 1) * P],
                rhs=w_codes[u][:].bitcast(FP8X4),
                rhs_scale=w_scales[u][:],
                start=(m == 0),
                stop=(m == 1),
            )

        stats = {}
        mean_var = {}
        rstd = {}
        centred = {}

        def norm_stats(n, v):
            stats[n] = kept.tile([P, 6], F32, name="stats_%d" % n)
            nc.vector.bn_stats(out=stats[n][:], in_=v)

        def norm_moments(n):
            mean_var[n] = kept.tile([P, 2], F32, name="mean_var_%d" % n)
            nc.vector.bn_aggr(out=mean_var[n][:], in_=stats[n][:])
            var = mean_var[n][:, 1:2]
            floor = kept.tile([P, 1], F32, name="floor_%d" % n)
            nc.gpsimd.tensor_scalar(
                out=floor[:], in0=var, scalar1=EPS, scalar2=VAR_FLOOR, op0=ALU.is_lt, op1=ALU.mult
            )
            padded = kept.tile([P, 1], F32, name="padded_%d" % n)
            nc.gpsimd.tensor_scalar(
                out=padded[:], in0=floor[:], scalar1=var, scalar2=EPS, op0=ALU.add, op1=ALU.add
            )
            rstd[n] = kept.tile([P, 1], F32, name="rstd_%d" % n)
            nc.gpsimd.tensor_tensor(out=rstd[n][:], in0=padded[:], in1=minus_half[:], op=ALU.pow)

        def norm_centre(n, v):
            centred[n] = kept.tile([P, H], F32, name="centred_%d" % n)
            nc.vector.scalar_tensor_tensor(
                out=centred[n][:], in0=v, scalar=mean_var[n][:, 0:1], in1=affine[n][:, 0:H],
                op0=ALU.subtract, op1=ALU.mult,
            )

        normed = {}

        def norm_finish(n, cols):
            if n not in normed:
                normed[n] = kept.tile([P, H], F32, name="normed_%d" % n)
            nc.vector.scalar_tensor_tensor(
                out=normed[n][:, cols], in0=centred[n][:, cols], scalar=rstd[n][:],
                in1=affine[n][:, H : 2 * H][:, cols], op0=ALU.mult, op1=ALU.add,
            )

        gate = {}

        def apply_function(g):
            gate[g] = kept.tile([P, H], F32, name="gate_%d" % g)
            nc.scalar.activation(
                out=gate[g][:], in_=normed[g][:], func=gate_func[g], bias=gate_bias[:, g : g + 1]
            )

        whole = slice(0, H)
        halves = (slice(0, H // 2), slice(H // 2, H))

        bank = new_bank()
        planes = bank[:].rearrange("p (u c) -> p u c", u=2)
        transpose_words(planes, 0, affine_rows[:].bitcast(F32))
        affine_cols = consts.tile([P, 2, 2 * NORMS], F32)
        nc.vector.tensor_copy(out=affine_cols[:], in_=planes[:, :, 0 : 2 * NORMS])

        bank = new_bank()
        planes = bank[:].rearrange("p (u c) -> p u c", u=2)
        transpose_words(planes, 0, x_rows[:].bitcast(F32))
        transpose_words(planes, P, hx_rows[:].bitcast(F32))
        act_grouped = staging.tile([P, 4 * 2 * P], BF16, align_bytes=64)
        regroup(act_grouped[:].bitcast(F32), planes)
        act_codes = operands.tile([P, 2 * P], U32, align_bytes=64)
        act_scales = operands.tile([P, 2 * P], U8, align_bytes=64)
        nc.vector.quantize_mx(
            out=act_codes[:].bitcast(FP8X4), scales=act_scales[:], in_=act_grouped[:]
        )

        for n in (I_GATE, F_GATE, G_GATE):
            spread_transposes(n)
        for n in (I_GATE, F_GATE, G_GATE):
            spread_copy(n, nc.vector.tensor_copy)

        for j in (I_GATE, F_GATE, G_GATE):
            for u in (2 * j, 2 * j + 1):
                unit_to_k_major(u)
                if u >= 2:
                    mx_pass(u - 2)
            quantise(2 * j)
            if j >= 1:
                norm_stats(j - 1, acc[j - 1][:])
            quantise(2 * j + 1)
            if j >= 1:
                norm_moments(j - 1)
            if j >= 2:
                norm_finish(j - 2, whole)
            if j >= 1:
                norm_centre(j - 1, acc[j - 1][:])

        unit_to_k_major(2 * O_GATE)
        mx_pass(2 * G_GATE)
        mx_pass(2 * G_GATE + 1)
        unit_to_k_major(2 * O_GATE + 1)
        for n in (O_GATE, CELL):
            spread_transposes(n)
            spread_copy(n, nc.scalar.copy)

        norm_stats(G_GATE, acc[G_GATE][:])
        quantise(2 * O_GATE)
        norm_moments(G_GATE)
        quantise(2 * O_GATE + 1)
        norm_centre(G_GATE, acc[G_GATE][:])
        norm_finish(F_GATE, whole)
        norm_finish(G_GATE, whole)
        mx_pass(2 * O_GATE)
        mx_pass(2 * O_GATE + 1)
        for g in (I_GATE, F_GATE, G_GATE):
            apply_function(g)

        norm_stats(O_GATE, acc[O_GATE][:])
        held = kept.tile([P, H], F32)
        nc.vector.tensor_tensor(out=held[:], in0=gate[F_GATE][:], in1=cx_rows[:], op=ALU.mult)
        fresh = kept.tile([P, H], F32)
        nc.vector.tensor_tensor(out=fresh[:], in0=gate[I_GATE][:], in1=gate[G_GATE][:], op=ALU.mult)
        norm_moments(O_GATE)
        cell = kept.tile([P, H], F32)
        nc.vector.tensor_tensor(out=cell[:], in0=held[:], in1=fresh[:], op=ALU.add)
        norm_stats(CELL, cell[:])
        norm_moments(CELL)
        norm_centre(O_GATE, acc[O_GATE][:])
        norm_centre(CELL, cell[:])
        norm_finish(O_GATE, whole)
        apply_function(O_GATE)

        tanh_cy = kept.tile([P, H], F32)
        hy = kept.tile([P, H], F32)
        for cols in halves:
            norm_finish(CELL, cols)
        nc.sync.dma_start(out=out_2[:, :], in_=normed[CELL][:])
        for cols in halves:
            nc.scalar.activation(out=tanh_cy[:, cols], in_=normed[CELL][:, cols], func=ACT.Tanh)
        for cols in halves:
            nc.vector.tensor_tensor(
                out=hy[:, cols], in0=gate[O_GATE][:, cols], in1=tanh_cy[:, cols], op=ALU.mult
            )
            nc.sync.dma_start(out=out_0[:, cols], in_=hy[:, cols])
            nc.sync.dma_start(out=out_1[:, cols], in_=hy[:, cols])
